import numpy as np
import ml_dtypes

BF16 = ml_dtypes.bfloat16


def bf(x):
    return np.asarray(x, np.float32).astype(BF16)


def f32(x):
    return np.asarray(x, np.float32)


def f64(x):
    return np.asarray(x).astype(np.float64)


def striped(idx):
    return np.tile(idx.reshape(-1, 16).T, (8, 1))


B, H, L, HD, S, R, N = 4, 128, 16, 16, 512, 256, 1024
SCALE = 1.0 / np.sqrt(HD)


def setup_inputs():
    return {"emb": f32(np.random.standard_normal((H, S))), "qk": f32(np.sqrt(HD) * np.random.standard_normal((H, N))), "offs": striped(np.concatenate([np.random.permutation(S)[:R] for _ in range(B)]))}


def reference(emb, qk, offs):
    idx = offs[:16].T.reshape(-1)
    s = f64(emb)[:, idx] + SCALE * f64(qk)
    s = s.reshape(H, B * L, L)
    e = np.exp(s - s.max(axis=-1, keepdims=True))
    return (e / e.sum(axis=-1, keepdims=True)).reshape(H, N)

@@ -1,0 +1,69 @@
+import concourse.mybir as mybir
+
+F32 = mybir.dt.float32
+U16 = mybir.dt.uint16
+ADD = mybir.AluOpType.add
+SUBTRACT = mybir.AluOpType.subtract
+MULT = mybir.AluOpType.mult
+MAX = mybir.AluOpType.max
+EXP = mybir.ActivationFunctionType.Exp
+X = mybir.AxisListType.X
+
+HEADS = 128
+CLASSES = 512
+N = 1024
+KEYS = 16
+PER_COLUMN = 16
+PIECE = 256
+PIECES = N // PIECE
+QUERIES = PIECE // KEYS
+SCALE = 0.25
+
+
+def tile_relmultiheadattention_kernel(tc, emb, qk, offs, out):
+    nc = tc.nc
+    with (
+        tc.tile_pool(name="held", bufs=1) as held,
+        tc.tile_pool(name="work", bufs=PIECES) as work,
+    ):
+        offsets = held.tile([HEADS, N // PER_COLUMN], U16, name="offsets")
+        nc.sync.dma_start(offsets[:], offs)
+        table = held.tile([HEADS, CLASSES], F32, name="table")
+        nc.sync.dma_start(table[:], emb)
+
+        for piece in range(PIECES):
+            columns = slice(piece * PIECE, (piece + 1) * PIECE)
+            piece_offsets = offsets[:, piece * (PIECE // PER_COLUMN) : (piece + 1) * (PIECE // PER_COLUMN)]
+
+            raw = work.tile([HEADS, PIECE], F32, name="raw")
+            nc.sync.dma_start(raw[:], qk[:, columns])
+            scaled = work.tile([HEADS, PIECE], F32, name="scaled")
+            nc.scalar.mul(scaled[:], raw[:], SCALE)
+
+            scores = work.tile([HEADS, PIECE], F32, name="scores")
+            nc.vector.tensor_tensor(scores[:], table[:].indirect(piece_offsets), scaled[:], ADD)
+
+            by_query = [HEADS, QUERIES, KEYS]
+            top = work.tile([HEADS, QUERIES], F32, name="top")
+            nc.vector.tensor_reduce(top[:], scores[:].rearrange("h (q k) -> h q k", k=KEYS), X, MAX)
+            shifted = work.tile([HEADS, PIECE], F32, name="shifted")
+            nc.vector.tensor_tensor(
+                shifted[:].rearrange("h (q k) -> h q k", k=KEYS),
+                scores[:].rearrange("h (q k) -> h q k", k=KEYS),
+                top[:].unsqueeze(2).to_broadcast(by_query),
+                SUBTRACT,
+            )
+            weights = work.tile([HEADS, PIECE], F32, name="weights")
+            nc.scalar.activation(weights[:], shifted[:], EXP)
+            total = work.tile([HEADS, QUERIES], F32, name="total")
+            nc.vector.tensor_reduce(total[:], weights[:].rearrange("h (q k) -> h q k", k=KEYS), X, ADD)
+            inverse = work.tile([HEADS, QUERIES], F32, name="inverse")
+            nc.vector.reciprocal(inverse[:], total[:])
+            normed = work.tile([HEADS, PIECE], F32, name="normed")
+            nc.vector.tensor_tensor(
+                normed[:].rearrange("h (q k) -> h q k", k=KEYS),
+                weights[:].rearrange("h (q k) -> h q k", k=KEYS),
+                inverse[:].unsqueeze(2).to_broadcast(by_query),
+                MULT,
+            )
+            nc.sync.dma_start(out[:, columns], normed[:])

@@ -47,7 +47,7 @@ def tile_relmultiheadattention_kernel(tc, emb, qk, offs, out):
             top = work.tile([HEADS, QUERIES], F32, name="top")
             nc.vector.tensor_reduce(top[:], scores[:].rearrange("h (q k) -> h q k", k=KEYS), X, MAX)
             shifted = work.tile([HEADS, PIECE], F32, name="shifted")
-            nc.vector.tensor_tensor(
+            nc.gpsimd.tensor_tensor(
                 shifted[:].rearrange("h (q k) -> h q k", k=KEYS),
                 scores[:].rearrange("h (q k) -> h q k", k=KEYS),
                 top[:].unsqueeze(2).to_broadcast(by_query),
@@ -60,7 +60,7 @@ def tile_relmultiheadattention_kernel(tc, emb, qk, offs, out):
             inverse = work.tile([HEADS, QUERIES], F32, name="inverse")
             nc.vector.reciprocal(inverse[:], total[:])
             normed = work.tile([HEADS, PIECE], F32, name="normed")
-            nc.vector.tensor_tensor(
+            nc.gpsimd.tensor_tensor(
                 normed[:].rearrange("h (q k) -> h q k", k=KEYS),
                 weights[:].rearrange("h (q k) -> h q k", k=KEYS),
                 inverse[:].unsqueeze(2).to_broadcast(by_query),

@@ -20,50 +20,51 @@ QUERIES = PIECE // KEYS
 SCALE = 0.25
 
 
+def by_query(tile):
+    return tile[:].rearrange("h (q k) -> h q k", k=KEYS)
+
+
+def over_keys(tile):
+    return tile[:].unsqueeze(2).to_broadcast([HEADS, QUERIES, KEYS])
+
+
 def tile_relmultiheadattention_kernel(tc, emb, qk, offs, out):
     nc = tc.nc
-    with (
-        tc.tile_pool(name="held", bufs=1) as held,
-        tc.tile_pool(name="work", bufs=PIECES) as work,
-    ):
+    pieces = range(PIECES)
+    with tc.tile_pool(name="held", bufs=1) as held:
         offsets = held.tile([HEADS, N // PER_COLUMN], U16, name="offsets")
         nc.sync.dma_start(offsets[:], offs)
         table = held.tile([HEADS, CLASSES], F32, name="table")
         nc.sync.dma_start(table[:], emb)
 
-        for piece in range(PIECES):
-            columns = slice(piece * PIECE, (piece + 1) * PIECE)
-            piece_offsets = offsets[:, piece * (PIECE // PER_COLUMN) : (piece + 1) * (PIECE // PER_COLUMN)]
+        def wide(name):
+            return [held.tile([HEADS, PIECE], F32, name=f"{name}{p}") for p in pieces]
 
-            raw = work.tile([HEADS, PIECE], F32, name="raw")
-            nc.sync.dma_start(raw[:], qk[:, columns])
-            scaled = work.tile([HEADS, PIECE], F32, name="scaled")
-            nc.scalar.mul(scaled[:], raw[:], SCALE)
+        def narrow(name):
+            return [held.tile([HEADS, QUERIES], F32, name=f"{name}{p}") for p in pieces]
 
-            scores = work.tile([HEADS, PIECE], F32, name="scores")
-            nc.vector.tensor_tensor(scores[:], table[:].indirect(piece_offsets), scaled[:], ADD)
+        raw, scaled, scores, shifted, weights, normed = (
+            wide(name) for name in ("raw", "scaled", "scores", "shifted", "weights", "normed")
+        )
+        top, total, inverse = (narrow(name) for name in ("top", "total", "inverse"))
 
-            by_query = [HEADS, QUERIES, KEYS]
-            top = work.tile([HEADS, QUERIES], F32, name="top")
-            nc.vector.tensor_reduce(top[:], scores[:].rearrange("h (q k) -> h q k", k=KEYS), X, MAX)
-            shifted = work.tile([HEADS, PIECE], F32, name="shifted")
-            nc.gpsimd.tensor_tensor(
-                shifted[:].rearrange("h (q k) -> h q k", k=KEYS),
-                scores[:].rearrange("h (q k) -> h q k", k=KEYS),
-                top[:].unsqueeze(2).to_broadcast(by_query),
-                SUBTRACT,
-            )
-            weights = work.tile([HEADS, PIECE], F32, name="weights")
-            nc.scalar.activation(weights[:], shifted[:], EXP)
-            total = work.tile([HEADS, QUERIES], F32, name="total")
-            nc.vector.tensor_reduce(total[:], weights[:].rearrange("h (q k) -> h q k", k=KEYS), X, ADD)
-            inverse = work.tile([HEADS, QUERIES], F32, name="inverse")
-            nc.vector.reciprocal(inverse[:], total[:])
-            normed = work.tile([HEADS, PIECE], F32, name="normed")
-            nc.gpsimd.tensor_tensor(
-                normed[:].rearrange("h (q k) -> h q k", k=KEYS),
-                weights[:].rearrange("h (q k) -> h q k", k=KEYS),
-                inverse[:].unsqueeze(2).to_broadcast(by_query),
-                MULT,
-            )
-            nc.sync.dma_start(out[:, columns], normed[:])
+        for p in pieces:
+            nc.scalar.dma_start(raw[p][:], qk[:, p * PIECE : (p + 1) * PIECE])
+        for p in pieces:
+            nc.scalar.mul(scaled[p][:], raw[p][:], SCALE)
+        for p in pieces:
+            piece_offsets = offsets[:, p * (PIECE // PER_COLUMN) : (p + 1) * (PIECE // PER_COLUMN)]
+            nc.vector.tensor_tensor(scores[p][:], table[:].indirect(piece_offsets), scaled[p][:], ADD)
+        for p in pieces:
+            nc.vector.tensor_reduce(top[p][:], by_query(scores[p]), X, MAX)
+        for p in pieces:
+            nc.vector.tensor_tensor(by_query(shifted[p]), by_query(scores[p]), over_keys(top[p]), SUBTRACT)
+        for p in pieces:
+            nc.scalar.activation(weights[p][:], shifted[p][:], EXP)
+        for p in pieces:
+            nc.vector.tensor_reduce(total[p][:], by_query(weights[p]), X, ADD)
+        for p in pieces:
+            nc.vector.reciprocal(inverse[p][:], total[p][:])
+        for p in pieces:
+            nc.vector.tensor_tensor(by_query(normed[p]), by_query(weights[p]), over_keys(inverse[p]), MULT)
+            nc.sync.dma_start(out[:, p * PIECE : (p + 1) * PIECE], normed[p][:])

@@ -3,7 +3,6 @@ import concourse.mybir as mybir
 F32 = mybir.dt.float32
 U16 = mybir.dt.uint16
 ADD = mybir.AluOpType.add
-SUBTRACT = mybir.AluOpType.subtract
 MULT = mybir.AluOpType.mult
 MAX = mybir.AluOpType.max
 EXP = mybir.ActivationFunctionType.Exp
@@ -30,41 +29,39 @@ def over_keys(tile):
 
 def tile_relmultiheadattention_kernel(tc, emb, qk, offs, out):
     nc = tc.nc
-    pieces = range(PIECES)
-    with tc.tile_pool(name="held", bufs=1) as held:
+    with (
+        tc.tile_pool(name="held", bufs=1) as held,
+        tc.tile_pool(name="work", bufs=PIECES) as work,
+    ):
         offsets = held.tile([HEADS, N // PER_COLUMN], U16, name="offsets")
         nc.sync.dma_start(offsets[:], offs)
         table = held.tile([HEADS, CLASSES], F32, name="table")
         nc.sync.dma_start(table[:], emb)
 
-        def wide(name):
-            return [held.tile([HEADS, PIECE], F32, name=f"{name}{p}") for p in pieces]
+        for p in range(PIECES):
+            columns = slice(p * PIECE, (p + 1) * PIECE)
+            raw = work.tile([HEADS, PIECE], F32, name="raw")
+            nc.scalar.dma_start(raw[:], qk[:, columns])
+            scaled = work.tile([HEADS, PIECE], F32, name="scaled")
+            nc.scalar.mul(scaled[:], raw[:], SCALE)
 
-        def narrow(name):
-            return [held.tile([HEADS, QUERIES], F32, name=f"{name}{p}") for p in pieces]
-
-        raw, scaled, scores, shifted, weights, normed = (
-            wide(name) for name in ("raw", "scaled", "scores", "shifted", "weights", "normed")
-        )
-        top, total, inverse = (narrow(name) for name in ("top", "total", "inverse"))
-
-        for p in pieces:
-            nc.scalar.dma_start(raw[p][:], qk[:, p * PIECE : (p + 1) * PIECE])
-        for p in pieces:
-            nc.scalar.mul(scaled[p][:], raw[p][:], SCALE)
-        for p in pieces:
             piece_offsets = offsets[:, p * (PIECE // PER_COLUMN) : (p + 1) * (PIECE // PER_COLUMN)]
-            nc.vector.tensor_tensor(scores[p][:], table[:].indirect(piece_offsets), scaled[p][:], ADD)
-        for p in pieces:
-            nc.vector.tensor_reduce(top[p][:], by_query(scores[p]), X, MAX)
-        for p in pieces:
-            nc.vector.tensor_tensor(by_query(shifted[p]), by_query(scores[p]), over_keys(top[p]), SUBTRACT)
-        for p in pieces:
-            nc.scalar.activation(weights[p][:], shifted[p][:], EXP)
-        for p in pieces:
-            nc.vector.tensor_reduce(total[p][:], by_query(weights[p]), X, ADD)
-        for p in pieces:
-            nc.vector.reciprocal(inverse[p][:], total[p][:])
-        for p in pieces:
-            nc.vector.tensor_tensor(by_query(normed[p]), by_query(weights[p]), over_keys(inverse[p]), MULT)
-            nc.sync.dma_start(out[:, p * PIECE : (p + 1) * PIECE], normed[p][:])
+            scores = work.tile([HEADS, PIECE], F32, name="scores")
+            nc.vector.tensor_tensor(scores[:], table[:].indirect(piece_offsets), scaled[:], ADD)
+
+            minus_top = work.tile([HEADS, QUERIES], F32, name="minus_top")
+            nc.vector.tensor_reduce(minus_top[:], by_query(scores), X, MAX, negate=True)
+
+            weights = work.tile([HEADS, PIECE], F32, name="weights")
+            total = work.tile([HEADS, QUERIES], F32, name="total")
+            for q in range(QUERIES):
+                keys = slice(q * KEYS, (q + 1) * KEYS)
+                nc.scalar.activation(
+                    weights[:, keys], scores[:, keys], EXP, bias=minus_top[:, q : q + 1], accum_out=total[:, q : q + 1]
+                )
+
+            inverse = work.tile([HEADS, QUERIES], F32, name="inverse")
+            nc.vector.reciprocal(inverse[:], total[:])
+            normed = work.tile([HEADS, PIECE], F32, name="normed")
+            nc.vector.tensor_tensor(by_query(normed), by_query(weights), over_keys(inverse), MULT)
+            nc.sync.dma_start(out[:, columns], normed[:])

@@ -3,6 +3,7 @@ import concourse.mybir as mybir
 F32 = mybir.dt.float32
 U16 = mybir.dt.uint16
 ADD = mybir.AluOpType.add
+SUBTRACT = mybir.AluOpType.subtract
 MULT = mybir.AluOpType.mult
 MAX = mybir.AluOpType.max
 EXP = mybir.ActivationFunctionType.Exp
@@ -29,39 +30,43 @@ def over_keys(tile):
 
 def tile_relmultiheadattention_kernel(tc, emb, qk, offs, out):
     nc = tc.nc
-    with (
-        tc.tile_pool(name="held", bufs=1) as held,
-        tc.tile_pool(name="work", bufs=PIECES) as work,
-    ):
+    pieces = range(PIECES)
+    with tc.tile_pool(name="held", bufs=1) as held:
         offsets = held.tile([HEADS, N // PER_COLUMN], U16, name="offsets")
         nc.sync.dma_start(offsets[:], offs)
         table = held.tile([HEADS, CLASSES], F32, name="table")
         nc.sync.dma_start(table[:], emb)
 
-        for p in range(PIECES):
-            columns = slice(p * PIECE, (p + 1) * PIECE)
-            raw = work.tile([HEADS, PIECE], F32, name="raw")
-            nc.scalar.dma_start(raw[:], qk[:, columns])
-            scaled = work.tile([HEADS, PIECE], F32, name="scaled")
-            nc.scalar.mul(scaled[:], raw[:], SCALE)
+        def wide(name):
+            return [held.tile([HEADS, PIECE], F32, name=f"{name}{p}") for p in pieces]
 
+        def narrow(name):
+            return [held.tile([HEADS, QUERIES], F32, name=f"{name}{p}") for p in pieces]
+
+        raw, scaled, scores, shifted, weights, normed = (
+            wide(name) for name in ("raw", "scaled", "scores", "shifted", "weights", "normed")
+        )
+        top, total, inverse = (narrow(name) for name in ("top", "total", "inverse"))
+
+        elementwise = [nc.gpsimd] + [nc.vector] * (PIECES - 1)
+
+        for p in pieces:
+            nc.scalar.dma_start(raw[p][:], qk[:, p * PIECE : (p + 1) * PIECE])
+        for p in pieces:
+            nc.scalar.mul(scaled[p][:], raw[p][:], SCALE)
+        for p in pieces:
             piece_offsets = offsets[:, p * (PIECE // PER_COLUMN) : (p + 1) * (PIECE // PER_COLUMN)]
-            scores = work.tile([HEADS, PIECE], F32, name="scores")
-            nc.vector.tensor_tensor(scores[:], table[:].indirect(piece_offsets), scaled[:], ADD)
-
-            minus_top = work.tile([HEADS, QUERIES], F32, name="minus_top")
-            nc.vector.tensor_reduce(minus_top[:], by_query(scores), X, MAX, negate=True)
-
-            weights = work.tile([HEADS, PIECE], F32, name="weights")
-            total = work.tile([HEADS, QUERIES], F32, name="total")
-            for q in range(QUERIES):
-                keys = slice(q * KEYS, (q + 1) * KEYS)
-                nc.scalar.activation(
-                    weights[:, keys], scores[:, keys], EXP, bias=minus_top[:, q : q + 1], accum_out=total[:, q : q + 1]
-                )
-
-            inverse = work.tile([HEADS, QUERIES], F32, name="inverse")
-            nc.vector.reciprocal(inverse[:], total[:])
-            normed = work.tile([HEADS, PIECE], F32, name="normed")
-            nc.vector.tensor_tensor(by_query(normed), by_query(weights), over_keys(inverse), MULT)
-            nc.sync.dma_start(out[:, columns], normed[:])
+            nc.vector.tensor_tensor(scores[p][:], table[:].indirect(piece_offsets), scaled[p][:], ADD)
+        for p in pieces:
+            nc.vector.tensor_reduce(top[p][:], by_query(scores[p]), X, MAX)
+        for p in pieces:
+            elementwise[p].tensor_tensor(by_query(shifted[p]), by_query(scores[p]), over_keys(top[p]), SUBTRACT)
+        for p in pieces:
+            nc.scalar.activation(weights[p][:], shifted[p][:], EXP)
+        for p in pieces:
+            nc.vector.tensor_reduce(total[p][:], by_query(weights[p]), X, ADD)
+        for p in pieces:
+            nc.vector.reciprocal(inverse[p][:], total[p][:])
+        for p in pieces:
+            elementwise[p].tensor_tensor(by_query(normed[p]), by_query(weights[p]), over_keys(inverse[p]), MULT)
+            nc.sync.dma_start(out[:, p * PIECE : (p + 1) * PIECE], normed[p][:])

@@ -3,7 +3,6 @@ import concourse.mybir as mybir
 F32 = mybir.dt.float32
 U16 = mybir.dt.uint16
 ADD = mybir.AluOpType.add
-SUBTRACT = mybir.AluOpType.subtract
 MULT = mybir.AluOpType.mult
 MAX = mybir.AluOpType.max
 EXP = mybir.ActivationFunctionType.Exp
@@ -43,30 +42,32 @@ def tile_relmultiheadattention_kernel(tc, emb, qk, offs, out):
         def narrow(name):
             return [held.tile([HEADS, QUERIES], F32, name=f"{name}{p}") for p in pieces]
 
-        raw, scaled, scores, shifted, weights, normed = (
-            wide(name) for name in ("raw", "scaled", "scores", "shifted", "weights", "normed")
+        raw, scaled, scores, weights, normed = (
+            wide(name) for name in ("raw", "scaled", "scores", "weights", "normed")
         )
-        top, total, inverse = (narrow(name) for name in ("top", "total", "inverse"))
-
-        elementwise = [nc.gpsimd] + [nc.vector] * (PIECES - 1)
+        minus_top, total, inverse = (narrow(name) for name in ("minus_top", "total", "inverse"))
 
         for p in pieces:
             nc.scalar.dma_start(raw[p][:], qk[:, p * PIECE : (p + 1) * PIECE])
         for p in pieces:
             nc.scalar.mul(scaled[p][:], raw[p][:], SCALE)
-        for p in pieces:
-            piece_offsets = offsets[:, p * (PIECE // PER_COLUMN) : (p + 1) * (PIECE // PER_COLUMN)]
-            nc.vector.tensor_tensor(scores[p][:], table[:].indirect(piece_offsets), scaled[p][:], ADD)
-        for p in pieces:
-            nc.vector.tensor_reduce(top[p][:], by_query(scores[p]), X, MAX)
-        for p in pieces:
-            elementwise[p].tensor_tensor(by_query(shifted[p]), by_query(scores[p]), over_keys(top[p]), SUBTRACT)
-        for p in pieces:
-            nc.scalar.activation(weights[p][:], shifted[p][:], EXP)
-        for p in pieces:
-            nc.vector.tensor_reduce(total[p][:], by_query(weights[p]), X, ADD)
-        for p in pieces:
-            nc.vector.reciprocal(inverse[p][:], total[p][:])
-        for p in pieces:
-            elementwise[p].tensor_tensor(by_query(normed[p]), by_query(weights[p]), over_keys(inverse[p]), MULT)
-            nc.sync.dma_start(out[:, p * PIECE : (p + 1) * PIECE], normed[p][:])
+
+        pairs = [(0, 1), (2, 3)]
+        for pair in pairs:
+            for p in pair:
+                piece_offsets = offsets[:, p * (PIECE // PER_COLUMN) : (p + 1) * (PIECE // PER_COLUMN)]
+                nc.vector.tensor_tensor(scores[p][:], table[:].indirect(piece_offsets), scaled[p][:], ADD)
+            for p in pair:
+                nc.vector.tensor_reduce(minus_top[p][:], by_query(scores[p]), X, MAX, negate=True)
+            for p in pair:
+                for q in range(QUERIES):
+                    keys = slice(q * KEYS, (q + 1) * KEYS)
+                    nc.scalar.activation(weights[p][:, keys], scores[p][:, keys], EXP, bias=minus_top[p][:, q : q + 1])
+        for pair in pairs:
+            for p in pair:
+                nc.vector.tensor_reduce(total[p][:], by_query(weights[p]), X, ADD)
+            for p in pair:
+                nc.vector.reciprocal(inverse[p][:], total[p][:])
+            for p in pair:
+                nc.vector.tensor_tensor(by_query(normed[p]), by_query(weights[p]), over_keys(inverse[p]), MULT)
+                nc.sync.dma_start(out[:, p * PIECE : (p + 1) * PIECE], normed[p][:])

@@ -13,10 +13,9 @@ CLASSES = 512
 N = 1024
 KEYS = 16
 PER_COLUMN = 16
-PIECE = 256
-PIECES = N // PIECE
-QUERIES = PIECE // KEYS
 SCALE = 0.25
+WIDTHS = (128, 128, 256, 256, 128, 128)
+assert sum(WIDTHS) == N
 
 
 def by_query(tile):
@@ -24,50 +23,47 @@ def by_query(tile):
 
 
 def over_keys(tile):
-    return tile[:].unsqueeze(2).to_broadcast([HEADS, QUERIES, KEYS])
+    return tile[:].unsqueeze(2).to_broadcast([HEADS, tile.shape[1], KEYS])
 
 
 def tile_relmultiheadattention_kernel(tc, emb, qk, offs, out):
     nc = tc.nc
-    pieces = range(PIECES)
+    pieces = range(len(WIDTHS))
+    starts = [sum(WIDTHS[:p]) for p in pieces]
     with tc.tile_pool(name="held", bufs=1) as held:
         offsets = held.tile([HEADS, N // PER_COLUMN], U16, name="offsets")
-        nc.sync.dma_start(offsets[:], offs)
         table = held.tile([HEADS, CLASSES], F32, name="table")
-        nc.sync.dma_start(table[:], emb)
 
         def wide(name):
-            return [held.tile([HEADS, PIECE], F32, name=f"{name}{p}") for p in pieces]
+            return [held.tile([HEADS, WIDTHS[p]], F32, name=f"{name}{p}") for p in pieces]
 
         def narrow(name):
-            return [held.tile([HEADS, QUERIES], F32, name=f"{name}{p}") for p in pieces]
+            return [held.tile([HEADS, WIDTHS[p] // KEYS], F32, name=f"{name}{p}") for p in pieces]
 
         raw, scaled, scores, weights, normed = (
             wide(name) for name in ("raw", "scaled", "scores", "weights", "normed")
         )
         minus_top, total, inverse = (narrow(name) for name in ("minus_top", "total", "inverse"))
 
+        def columns(p):
+            return slice(starts[p], starts[p] + WIDTHS[p])
+
+        nc.sync.dma_start(offsets[:], offs)
+        nc.sync.dma_start(table[:], emb)
         for p in pieces:
-            nc.scalar.dma_start(raw[p][:], qk[:, p * PIECE : (p + 1) * PIECE])
+            nc.scalar.dma_start(raw[p][:], qk[:, columns(p)])
         for p in pieces:
             nc.scalar.mul(scaled[p][:], raw[p][:], SCALE)
 
-        pairs = [(0, 1), (2, 3)]
-        for pair in pairs:
-            for p in pair:
-                piece_offsets = offsets[:, p * (PIECE // PER_COLUMN) : (p + 1) * (PIECE // PER_COLUMN)]
-                nc.vector.tensor_tensor(scores[p][:], table[:].indirect(piece_offsets), scaled[p][:], ADD)
-            for p in pair:
-                nc.vector.tensor_reduce(minus_top[p][:], by_query(scores[p]), X, MAX, negate=True)
-            for p in pair:
-                for q in range(QUERIES):
-                    keys = slice(q * KEYS, (q + 1) * KEYS)
-                    nc.scalar.activation(weights[p][:, keys], scores[p][:, keys], EXP, bias=minus_top[p][:, q : q + 1])
-        for pair in pairs:
-            for p in pair:
-                nc.vector.tensor_reduce(total[p][:], by_query(weights[p]), X, ADD)
-            for p in pair:
-                nc.vector.reciprocal(inverse[p][:], total[p][:])
-            for p in pair:
-                nc.vector.tensor_tensor(by_query(normed[p]), by_query(weights[p]), over_keys(inverse[p]), MULT)
-                nc.sync.dma_start(out[:, p * PIECE : (p + 1) * PIECE], normed[p][:])
+        for p in pieces:
+            piece_offsets = offsets[:, starts[p] // PER_COLUMN : (starts[p] + WIDTHS[p]) // PER_COLUMN]
+            nc.vector.tensor_tensor(scores[p][:], table[:].indirect(piece_offsets), scaled[p][:], ADD)
+            nc.vector.tensor_reduce(minus_top[p][:], by_query(scores[p]), X, MAX, negate=True)
+            for q in range(WIDTHS[p] // KEYS):
+                keys = slice(q * KEYS, (q + 1) * KEYS)
+                nc.scalar.activation(weights[p][:, keys], scores[p][:, keys], EXP, bias=minus_top[p][:, q : q + 1])
+        for p in pieces:
+            nc.vector.tensor_reduce(total[p][:], by_query(weights[p]), X, ADD)
+            nc.vector.reciprocal(inverse[p][:], total[p][:])
+            nc.vector.tensor_tensor(by_query(normed[p]), by_query(weights[p]), over_keys(inverse[p]), MULT)
+            nc.sync.dma_start(out[:, columns(p)], normed[p][:])

@@ -53,7 +53,10 @@ def tile_relmultiheadattention_kernel(tc, emb, qk, offs, out):
         for p in pieces:
             nc.scalar.dma_start(raw[p][:], qk[:, columns(p)])
         for p in pieces:
-            nc.scalar.mul(scaled[p][:], raw[p][:], SCALE)
+            if starts[p] < N // 4:
+                nc.vector.tensor_scalar_mul(scaled[p][:], raw[p][:], SCALE)
+            else:
+                nc.scalar.mul(scaled[p][:], raw[p][:], SCALE)
 
         for p in pieces:
             piece_offsets = offsets[:, starts[p] // PER_COLUMN : (starts[p] + WIDTHS[p]) // PER_COLUMN]

@@ -58,6 +58,7 @@ def tile_relmultiheadattention_kernel(tc, emb, qk, offs, out):
             else:
                 nc.scalar.mul(scaled[p][:], raw[p][:], SCALE)
 
+        on_scalar = (3,)
         for p in pieces:
             piece_offsets = offsets[:, starts[p] // PER_COLUMN : (starts[p] + WIDTHS[p]) // PER_COLUMN]
             nc.vector.tensor_tensor(scores[p][:], table[:].indirect(piece_offsets), scaled[p][:], ADD)
@@ -68,5 +69,10 @@ def tile_relmultiheadattention_kernel(tc, emb, qk, offs, out):
         for p in pieces:
             nc.vector.tensor_reduce(total[p][:], by_query(weights[p]), X, ADD)
             nc.vector.reciprocal(inverse[p][:], total[p][:])
-            nc.vector.tensor_tensor(by_query(normed[p]), by_query(weights[p]), over_keys(inverse[p]), MULT)
+            if p in on_scalar:
+                for q in range(WIDTHS[p] // KEYS):
+                    keys = slice(q * KEYS, (q + 1) * KEYS)
+                    nc.scalar.mul(normed[p][:, keys], weights[p][:, keys], inverse[p][:, q : q + 1])
+            else:
+                nc.vector.tensor_tensor(by_query(normed[p]), by_query(weights[p]), over_keys(inverse[p]), MULT)
             nc.sync.dma_start(out[:, columns(p)], normed[p][:])

@@ -48,8 +48,8 @@ def tile_relmultiheadattention_kernel(tc, emb, qk, offs, out):
         def columns(p):
             return slice(starts[p], starts[p] + WIDTHS[p])
 
-        nc.sync.dma_start(offsets[:], offs)
         nc.sync.dma_start(table[:], emb)
+        nc.sync.dma_start(offsets[:], offs)
         for p in pieces:
             nc.scalar.dma_start(raw[p][:], qk[:, columns(p)])
         for p in pieces:

import concourse.mybir as mybir

F32 = mybir.dt.float32
U16 = mybir.dt.uint16
ADD = mybir.AluOpType.add
MULT = mybir.AluOpType.mult
MAX = mybir.AluOpType.max
EXP = mybir.ActivationFunctionType.Exp
X = mybir.AxisListType.X

HEADS = 128
CLASSES = 512
N = 1024
KEYS = 16
PER_COLUMN = 16
SCALE = 0.25
WIDTHS = (128, 128, 256, 256, 128, 128)
assert sum(WIDTHS) == N


def by_query(tile):
    return tile[:].rearrange("h (q k) -> h q k", k=KEYS)


def over_keys(tile):
    return tile[:].unsqueeze(2).to_broadcast([HEADS, tile.shape[1], KEYS])


def tile_relmultiheadattention_kernel(tc, emb, qk, offs, out):
    nc = tc.nc
    pieces = range(len(WIDTHS))
    starts = [sum(WIDTHS[:p]) for p in pieces]
    with tc.tile_pool(name="held", bufs=1) as held:
        offsets = held.tile([HEADS, N // PER_COLUMN], U16, name="offsets")
        table = held.tile([HEADS, CLASSES], F32, name="table")

        def wide(name):
            return [held.tile([HEADS, WIDTHS[p]], F32, name=f"{name}{p}") for p in pieces]

        def narrow(name):
            return [held.tile([HEADS, WIDTHS[p] // KEYS], F32, name=f"{name}{p}") for p in pieces]

        raw, scaled, scores, weights, normed = (
            wide(name) for name in ("raw", "scaled", "scores", "weights", "normed")
        )
        minus_top, total, inverse = (narrow(name) for name in ("minus_top", "total", "inverse"))

        def columns(p):
            return slice(starts[p], starts[p] + WIDTHS[p])

        nc.sync.dma_start(table[:], emb)
        nc.sync.dma_start(offsets[:], offs)
        for p in pieces:
            nc.scalar.dma_start(raw[p][:], qk[:, columns(p)])
        for p in pieces:
            if starts[p] < N // 4:
                nc.vector.tensor_scalar_mul(scaled[p][:], raw[p][:], SCALE)
            else:
                nc.scalar.mul(scaled[p][:], raw[p][:], SCALE)

        on_scalar = (3,)
        for p in pieces:
            piece_offsets = offsets[:, starts[p] // PER_COLUMN : (starts[p] + WIDTHS[p]) // PER_COLUMN]
            nc.vector.tensor_tensor(scores[p][:], table[:].indirect(piece_offsets), scaled[p][:], ADD)
            nc.vector.tensor_reduce(minus_top[p][:], by_query(scores[p]), X, MAX, negate=True)
            for q in range(WIDTHS[p] // KEYS):
                keys = slice(q * KEYS, (q + 1) * KEYS)
                nc.scalar.activation(weights[p][:, keys], scores[p][:, keys], EXP, bias=minus_top[p][:, q : q + 1])
        for p in pieces:
            nc.vector.tensor_reduce(total[p][:], by_query(weights[p]), X, ADD)
            nc.vector.reciprocal(inverse[p][:], total[p][:])
            if p in on_scalar:
                for q in range(WIDTHS[p] // KEYS):
                    keys = slice(q * KEYS, (q + 1) * KEYS)
                    nc.scalar.mul(normed[p][:, keys], weights[p][:, keys], inverse[p][:, q : q + 1])
            else:
                nc.vector.tensor_tensor(by_query(normed[p]), by_query(weights[p]), over_keys(inverse[p]), MULT)
            nc.sync.dma_start(out[:, columns(p)], normed[p][:])
